import numpy as np
import ml_dtypes


def mxq(x, axis, fmt="e4m3"):
    dtype, down = {"e4m3": (ml_dtypes.float8_e4m3fn, 7), "e5m2": (ml_dtypes.float8_e5m2, 14)}[fmt]
    v = np.moveaxis(np.asarray(x, np.float32).astype(ml_dtypes.bfloat16).astype(np.float64), axis, -1)
    blocks = v.reshape(v.shape[:-1] + (-1, 32))
    amax = np.abs(blocks).max(-1, keepdims=True)
    byte = np.maximum(np.where(amax > 0, np.frexp(amax)[1] - 1 + 127, 0) - down, 1)
    scale = np.exp2(byte - 127.0)
    codes = (blocks / scale).astype(np.float32).astype(dtype).astype(np.float64)
    return np.moveaxis((codes * scale).reshape(v.shape), -1, axis)


WIDE = False


def mx_kscale(k):
    if not WIDE:
        return np.ones(k)
    levels = np.array([10, -10, 5, -5, 0])
    a = np.random.permutation(np.resize(levels, k // 512 * 4)).reshape(k // 512, 4)
    idx = np.arange(k)
    return np.exp2(a[idx // 512, idx % 128 // 32])


BF16 = ml_dtypes.bfloat16


def bf(x):
    return np.asarray(x, np.float32).astype(BF16)


def f64(x):
    return np.asarray(x).astype(np.float64)


E2M1 = np.array([0.0, 0.5, 1.0, 1.5, 2.0, 3.0, 4.0, 6.0, -0.0, -0.5, -1.0, -1.5, -2.0, -3.0, -4.0, -6.0])


def pack_weight(w, fmt):
    k, n = w.shape
    w = f64(bf(w)).reshape(k // 32, 32, n)
    amax = np.abs(w).max(1)
    if fmt == "e4m3":
        byte = np.frexp(amax)[1] - 1 + 127 - 7
    else:
        mant, ex = np.frexp(amax / 6.0)
        byte = np.where(mant > 0.5, ex, ex - 1) + 127
    byte = np.clip(np.where(amax > 0, byte, 1), 1, 254)
    scaled = (w * np.exp2(127.0 - byte)[:, None, :]).reshape(k, n).astype(np.float32)
    by_word = np.ascontiguousarray(scaled.reshape(k // 512, 128, 4, n).transpose(0, 1, 3, 2))
    if fmt == "e4m3":
        words = by_word.astype(ml_dtypes.float8_e4m3fn).view(np.uint8)
    else:
        c = by_word.astype(ml_dtypes.float4_e2m1fn).view(np.uint8) & 0xF
        words = c[..., 0::2] | (c[..., 1::2] << 4)
    return np.ascontiguousarray(words), np.ascontiguousarray(byte.astype(np.uint8).reshape(k // 512, 16, n))


def unpack_weight(words, scales, fmt):
    g, p, n, _ = words.shape
    if fmt == "e4m3":
        vals = np.ascontiguousarray(words).view(ml_dtypes.float8_e4m3fn).astype(np.float64)
    else:
        nib = np.empty((g, p, n, 4), np.uint8)
        nib[..., 0::2] = words & 0xF
        nib[..., 1::2] = words >> 4
        vals = E2M1[nib]
    vals = vals * np.repeat(np.exp2(scales.astype(np.float64) - 127.0), 8, axis=1)[..., None]
    return vals.transpose(0, 1, 3, 2).reshape(g * 512, n)

def pack4(w):
    words, scales = pack_weight(w, "e2m1")
    return words.reshape(words.shape[0], 128, -1), scales


def unpack4(words, scales):
    return unpack_weight(words.reshape(words.shape[0], 128, -1, 2), scales, "e2m1")


B, S, IN, OUT = 2, 256, 4096, 1024


def setup_inputs():
    s = mx_kscale(IN)
    input_ = bf(np.random.standard_normal((B, S, IN)) * s)
    weight = np.random.standard_normal((OUT, IN)) * (IN ** -0.5) / s[None, :]
    weight_words, weight_scales = pack4(np.ascontiguousarray(weight.T))
    bias = bf(np.random.standard_normal(OUT) * 0.1)
    return {"input_": input_,
            "weight_words": weight_words,
            "weight_scales": weight_scales,
            "bias": bias}


def reference(input_, weight_words, weight_scales, bias):
    xq = mxq(f64(input_), 2, "e4m3")
    wt = unpack4(weight_words, weight_scales)
    out = xq @ wt
    return out + f64(bias)

@@ -1,0 +1,145 @@
+from contextlib import ExitStack
+
+import concourse.mybir as mybir
+from concourse.masks import make_identity
+
+F32 = mybir.dt.float32
+BF16 = mybir.dt.bfloat16
+U8 = mybir.dt.uint8
+U32 = mybir.dt.uint32
+I32 = mybir.dt.int32
+FP8X4 = mybir.dt.float8_e4m3fn_x4
+FP4X4 = mybir.dt.float4_e2m1fn_x4
+ADD = mybir.AluOpType.add
+
+P = 128
+TOKENS = 512
+K = 4096
+N = 1024
+NH = 512
+FLOPS = 2 * TOKENS * K * N
+
+
+def tile_terowparallellinear_kernel(tc, input_, weight_words, weight_scales, bias, out):
+    nc = tc.nc
+    x = input_.flatten_outer_dims()
+    y = out.flatten_outer_dims()
+    scale_rows = weight_scales.rearrange("g q n -> q g n")
+
+    with ExitStack() as ctx:
+        keep = ctx.enter_context(tc.tile_pool(name="keep", bufs=1))
+        psum = ctx.enter_context(tc.psum_pool(name="psum", bufs=1))
+        ctx.enter_context(tc.manual_schedule())
+
+        planes = [keep.tile([P, 4, N], U8, name="w_planes_%d" % s, align_bytes=64) for s in range(2)]
+        bias_row = keep.tile([P, N], BF16, name="bias_row")
+        bias_all = keep.tile([P, N], F32, name="bias_all")
+        ones = keep.tile([P, P], BF16, name="ones")
+        ident = keep.tile([P, P], F32, name="ident")
+        nc.vector.memset(planes[0][:].rearrange("p g n -> p (g n)").bitcast(I32), 0)
+        nc.vector.memset(bias_row[:], 0.0)
+        nc.vector.memset(planes[1][:].rearrange("p g n -> p (g n)").bitcast(I32), 0)
+        nc.vector.memset(ones[:], 1.0)
+        make_identity(nc, ident[:])
+
+        x_sb = [[keep.tile([P, K // 2], BF16, name="x_%d_%d" % (m, s)) for s in range(2)] for m in range(4)]
+        w_words = [keep.tile([P, 2 * N], U8, name="w_words_%d" % g, align_bytes=64) for g in range(8)]
+
+        def load_x(m, s):
+            nc.sync.dma_start(out=x_sb[m][s][:], in_=x[P * m : P * (m + 1), (K // 2) * s : (K // 2) * (s + 1)])
+
+        def load_w(g):
+            nc.sync.dma_start(out=w_words[g][:].bitcast(I32), in_=weight_words[g].bitcast(I32))
+
+        def load_scales(s):
+            for r in range(4):
+                nc.sync.dma_start(
+                    out=planes[s][r:P:32, :, :].bitcast(I32),
+                    in_=scale_rows[r:16:4, 4 * s : 4 * s + 4, :].bitcast(I32),
+                )
+
+        nc.scalar.dma_start(out=bias_row[0:1, :], in_=bias.rearrange("(o n) -> o n", o=1))
+        load_x(0, 0)
+        load_x(1, 0)
+        load_scales(0)
+        for g in range(4):
+            load_w(g)
+        load_x(0, 1)
+        load_x(1, 1)
+        load_scales(1)
+        for g in range(4, 8):
+            load_w(g)
+        for m in (2, 3):
+            load_x(m, 0)
+            load_x(m, 1)
+
+        codes = [[None] * 4 for m in range(4)]
+        x_planes = [[None] * 4 for m in range(4)]
+        acc = [[None] * 2 for m in range(4)]
+
+        def quantise_half(m, s, first_bank):
+            words = x_sb[m][s][:].bitcast(F32)
+            for jj in range(2):
+                j = 2 * s + jj
+                bank = psum.tile([P, 2, 2, P], F32, tag="t%d" % (first_bank + jj), name="xt_%d_%d" % (m, j))
+                for gg in range(2):
+                    for u in range(2):
+                        c0 = 256 * (2 * jj + gg)
+                        nc.tensor.transpose(bank[:, gg, u, :], words[:, c0 + u : c0 + 256 : 2], ident[:])
+                grouped = keep.tile([P, 2, P, 4], BF16, name="grouped_%d_%d" % (m, j), align_bytes=64)
+                nc.scalar.copy(out=grouped[:].bitcast(F32), in_=bank[:].rearrange("p g u r -> p g r u"))
+                codes[m][j] = keep.tile([P, 2, P], U32, name="codes_%d_%d" % (m, j), align_bytes=64)
+                x_planes[m][j] = keep.tile([P, 2, P], U8, name="x_planes_%d_%d" % (m, j), align_bytes=64)
+                nc.vector.quantize_mx(
+                    out=codes[m][j][:].rearrange("p g r -> p (g r)").bitcast(FP8X4),
+                    scales=x_planes[m][j][:].rearrange("p g r -> p (g r)"),
+                    in_=grouped[:].rearrange("p g r t -> p (g r t)"),
+                )
+
+        def mx_pass(m, h, g):
+            if g == 0:
+                acc[m][h] = psum.tile([P, NH], F32, tag="a%d" % (2 * (m % 2) + h), name="acc_%d_%d" % (m, h))
+            nc.tensor.matmul_mx(
+                out=acc[m][h][:],
+                lhsT=codes[m][g // 2][:, g % 2, :].bitcast(FP8X4),
+                lhsT_scale=x_planes[m][g // 2][:, g % 2, :],
+                rhs=w_words[g][:, 2 * NH * h : 2 * NH * (h + 1)].bitcast(FP4X4),
+                rhs_scale=planes[g // 4][:, g % 4, NH * h : NH * (h + 1)],
+                start=(g == 0),
+                stop=(g == 7),
+            )
+
+        def finish(m, h):
+            result = keep.tile([P, NH], F32, name="result_%d_%d" % (m, h))
+            nc.vector.tensor_tensor(out=result[:], in0=acc[m][h][:], in1=bias_all[:, NH * h : NH * (h + 1)], op=ADD)
+            nc.sync.dma_start(out=y[P * m : P * (m + 1), NH * h : NH * (h + 1)], in_=result[:])
+
+        quantise_half(0, 0, 0)
+        quantise_half(1, 0, 2)
+        for g in range(4):
+            for m in (0, 1):
+                for h in range(2):
+                    mx_pass(m, h, g)
+        for h in range(2):
+            spread = psum.tile([P, NH], F32, tag="t%d" % h, name="spread_%d" % h)
+            nc.tensor.matmul(out=spread[:], lhsT=ones[:], rhs=bias_row[:, NH * h : NH * (h + 1)], start=True, stop=True)
+            if h == 0:
+                nc.scalar.copy(out=bias_all[:, 0:NH], in_=spread[:])
+            else:
+                nc.vector.tensor_copy(out=bias_all[:, NH : 2 * NH], in_=spread[:])
+        quantise_half(0, 1, 2)
+        quantise_half(1, 1, 0)
+        for m in (0, 1):
+            for h in range(2):
+                for g in range(4, 8):
+                    mx_pass(m, h, g)
+                finish(m, h)
+        quantise_half(2, 0, 2)
+        quantise_half(2, 1, 0)
+        quantise_half(3, 0, 2)
+        quantise_half(3, 1, 0)
+        for m in (2, 3):
+            for h in range(2):
+                for g in range(8):
+                    mx_pass(m, h, g)
+                finish(m, h)

@@ -73,11 +73,20 @@ def tile_terowparallellinear_kernel(tc, input_, weight_words, weight_scales, bia
             load_x(m, 0)
             load_x(m, 1)
 
+        ordered = [[None] * 2 for m in range(4)]
+        grouped = [[None] * 4 for m in range(4)]
         codes = [[None] * 4 for m in range(4)]
         x_planes = [[None] * 4 for m in range(4)]
         acc = [[None] * 2 for m in range(4)]
 
-        def quantise_half(m, s, first_bank):
+        def sort_half(m, s):
+            ordered[m][s] = keep.tile([P, 4, 2, P], F32, name="ordered_%d_%d" % (m, s))
+            nc.vector.tensor_copy(
+                out=ordered[m][s][:],
+                in_=x_sb[m][s][:].bitcast(F32).rearrange("p (g j u) -> p g u j", j=P, u=2),
+            )
+
+        def transpose_half(m, s, first_bank):
             words = x_sb[m][s][:].bitcast(F32)
             for jj in range(2):
                 j = 2 * s + jj
@@ -85,16 +94,21 @@ def tile_terowparallellinear_kernel(tc, input_, weight_words, weight_scales, bia
                 for gg in range(2):
                     for u in range(2):
                         c0 = 256 * (2 * jj + gg)
-                        nc.tensor.transpose(bank[:, gg, u, :], words[:, c0 + u : c0 + 256 : 2], ident[:])
-                grouped = keep.tile([P, 2, P, 4], BF16, name="grouped_%d_%d" % (m, j), align_bytes=64)
-                nc.scalar.copy(out=grouped[:].bitcast(F32), in_=bank[:].rearrange("p g u r -> p g r u"))
-                codes[m][j] = keep.tile([P, 2, P], U32, name="codes_%d_%d" % (m, j), align_bytes=64)
-                x_planes[m][j] = keep.tile([P, 2, P], U8, name="x_planes_%d_%d" % (m, j), align_bytes=64)
-                nc.vector.quantize_mx(
-                    out=codes[m][j][:].rearrange("p g r -> p (g r)").bitcast(FP8X4),
-                    scales=x_planes[m][j][:].rearrange("p g r -> p (g r)"),
-                    in_=grouped[:].rearrange("p g r t -> p (g r t)"),
-                )
+                        if ordered[m][s] is None:
+                            nc.tensor.transpose(bank[:, gg, u, :], words[:, c0 + u : c0 + 256 : 2], ident[:])
+                        else:
+                            nc.tensor.transpose(bank[:, gg, u, :], ordered[m][s][:, 2 * jj + gg, u, :], ident[:])
+                grouped[m][j] = keep.tile([P, 2, P, 4], BF16, name="grouped_%d_%d" % (m, j), align_bytes=64)
+                nc.scalar.copy(out=grouped[m][j][:].bitcast(F32), in_=bank[:].rearrange("p g u r -> p g r u"))
+
+        def quantise(m, j):
+            codes[m][j] = keep.tile([P, 2, P], U32, name="codes_%d_%d" % (m, j), align_bytes=64)
+            x_planes[m][j] = keep.tile([P, 2, P], U8, name="x_planes_%d_%d" % (m, j), align_bytes=64)
+            nc.vector.quantize_mx(
+                out=codes[m][j][:].rearrange("p g r -> p (g r)").bitcast(FP8X4),
+                scales=x_planes[m][j][:].rearrange("p g r -> p (g r)"),
+                in_=grouped[m][j][:].rearrange("p g r t -> p (g r t)"),
+            )
 
         def mx_pass(m, h, g):
             if g == 0:
@@ -114,12 +128,24 @@ def tile_terowparallellinear_kernel(tc, input_, weight_words, weight_scales, bia
             nc.vector.tensor_tensor(out=result[:], in0=acc[m][h][:], in1=bias_all[:, NH * h : NH * (h + 1)], op=ADD)
             nc.sync.dma_start(out=y[P * m : P * (m + 1), NH * h : NH * (h + 1)], in_=result[:])
 
-        quantise_half(0, 0, 0)
-        quantise_half(1, 0, 2)
+        def group(m, h, first, last):
+            for g in range(first, last):
+                mx_pass(m, h, g)
+            if last == 8:
+                finish(m, h)
+
+        transpose_half(0, 0, 0)
+        quantise(0, 0)
+        quantise(0, 1)
+        transpose_half(1, 0, 2)
+        quantise(1, 0)
+        quantise(1, 1)
         for g in range(4):
             for m in (0, 1):
                 for h in range(2):
                     mx_pass(m, h, g)
+        sort_half(0, 1)
+        sort_half(1, 1)
         for h in range(2):
             spread = psum.tile([P, NH], F32, tag="t%d" % h, name="spread_%d" % h)
             nc.tensor.matmul(out=spread[:], lhsT=ones[:], rhs=bias_row[:, NH * h : NH * (h + 1)], start=True, stop=True)
@@ -127,19 +153,31 @@ def tile_terowparallellinear_kernel(tc, input_, weight_words, weight_scales, bia
                 nc.scalar.copy(out=bias_all[:, 0:NH], in_=spread[:])
             else:
                 nc.vector.tensor_copy(out=bias_all[:, NH : 2 * NH], in_=spread[:])
-        quantise_half(0, 1, 2)
-        quantise_half(1, 1, 0)
-        for m in (0, 1):
-            for h in range(2):
-                for g in range(4, 8):
-                    mx_pass(m, h, g)
-                finish(m, h)
-        quantise_half(2, 0, 2)
-        quantise_half(2, 1, 0)
-        quantise_half(3, 0, 2)
-        quantise_half(3, 1, 0)
-        for m in (2, 3):
-            for h in range(2):
-                for g in range(8):
-                    mx_pass(m, h, g)
-                finish(m, h)
+        transpose_half(0, 1, 2)
+        quantise(0, 2)
+        quantise(0, 3)
+        transpose_half(1, 1, 0)
+        quantise(1, 2)
+        quantise(1, 3)
+        group(0, 0, 4, 8)
+        group(0, 1, 4, 8)
+        sort_half(2, 0)
+        group(1, 0, 4, 8)
+        sort_half(2, 1)
+        group(1, 1, 4, 8)
+        sort_half(3, 0)
+        transpose_half(2, 0, 2)
+        transpose_half(2, 1, 0)
+        transpose_half(3, 0, 2)
+        for j in range(4):
+            quantise(2, j)
+        sort_half(3, 1)
+        quantise(3, 0)
+        quantise(3, 1)
+        group(2, 0, 0, 8)
+        transpose_half(3, 1, 0)
+        quantise(3, 2)
+        quantise(3, 3)
+        group(2, 1, 0, 8)
+        group(3, 0, 0, 8)
+        group(3, 1, 0, 8)

@@ -31,153 +31,325 @@ def tile_terowparallellinear_kernel(tc, input_, weight_words, weight_scales, bia
         psum = ctx.enter_context(tc.psum_pool(name="psum", bufs=1))
         ctx.enter_context(tc.manual_schedule())
 
-        planes = [keep.tile([P, 4, N], U8, name="w_planes_%d" % s, align_bytes=64) for s in range(2)]
+        pieces = [[[0],[1],[2,3]],[[0],[1],[2,3]],[[0,1],[2,3]],[[0,1],[2,3]]]
+        plane_groups = [[0,2],[2,4],[4,8]]
+        where = {}
+        for m in range(4):
+            for i in range(len(pieces[m])):
+                for jj in range(len(pieces[m][i])):
+                    where[(m, pieces[m][i][jj])] = (i, jj)
+        plane_of = {}
+        for s in range(len(plane_groups)):
+            for g in range(plane_groups[s][0], plane_groups[s][1]):
+                plane_of[g] = (s, g - plane_groups[s][0])
+
+        planes = [keep.tile([P, r[1] - r[0], N], U8, name="w_planes_%d" % r[0], align_bytes=64) for r in plane_groups]
         bias_row = keep.tile([P, N], BF16, name="bias_row")
         bias_all = keep.tile([P, N], F32, name="bias_all")
         ones = keep.tile([P, P], BF16, name="ones")
         ident = keep.tile([P, P], F32, name="ident")
-        nc.vector.memset(planes[0][:].rearrange("p g n -> p (g n)").bitcast(I32), 0)
-        nc.vector.memset(bias_row[:], 0.0)
-        nc.vector.memset(planes[1][:].rearrange("p g n -> p (g n)").bitcast(I32), 0)
-        nc.vector.memset(ones[:], 1.0)
-        make_identity(nc, ident[:])
-
-        x_sb = [[keep.tile([P, K // 2], BF16, name="x_%d_%d" % (m, s)) for s in range(2)] for m in range(4)]
         w_words = [keep.tile([P, 2 * N], U8, name="w_words_%d" % g, align_bytes=64) for g in range(8)]
+        x_sb = {}
+        ordered = {}
+        banks = {}
+        grouped = {}
+        codes = {}
+        x_planes = {}
+        acc = {}
+        result = {}
 
-        def load_x(m, s):
-            nc.sync.dma_start(out=x_sb[m][s][:], in_=x[P * m : P * (m + 1), (K // 2) * s : (K // 2) * (s + 1)])
+        def zero_planes(s):
+            nc.vector.memset(planes[s][:].rearrange("p g n -> p (g n)").bitcast(I32), 0)
+
+        def load_x(m, i, queue):
+            js = pieces[m][i]
+            x_sb[(m, i)] = keep.tile([P, 1024 * len(js)], BF16, name="x_%d_%d" % (m, i))
+            queue.dma_start(out=x_sb[(m, i)][:], in_=x[P * m : P * (m + 1), 1024 * js[0] : 1024 * (js[-1] + 1)])
 
         def load_w(g):
             nc.sync.dma_start(out=w_words[g][:].bitcast(I32), in_=weight_words[g].bitcast(I32))
 
-        def load_scales(s):
+        def load_scales(s, queue, view):
+            g0, g1 = plane_groups[s]
             for r in range(4):
-                nc.sync.dma_start(
-                    out=planes[s][r:P:32, :, :].bitcast(I32),
-                    in_=scale_rows[r:16:4, 4 * s : 4 * s + 4, :].bitcast(I32),
-                )
+                queue.dma_start(out=planes[s][r:P:32, :, :].bitcast(view), in_=scale_rows[r:16:4, g0:g1, :].bitcast(view))
 
-        nc.scalar.dma_start(out=bias_row[0:1, :], in_=bias.rearrange("(o n) -> o n", o=1))
-        load_x(0, 0)
-        load_x(1, 0)
-        load_scales(0)
-        for g in range(4):
-            load_w(g)
-        load_x(0, 1)
-        load_x(1, 1)
-        load_scales(1)
-        for g in range(4, 8):
-            load_w(g)
-        for m in (2, 3):
-            load_x(m, 0)
-            load_x(m, 1)
-
-        ordered = [[None] * 2 for m in range(4)]
-        grouped = [[None] * 4 for m in range(4)]
-        codes = [[None] * 4 for m in range(4)]
-        x_planes = [[None] * 4 for m in range(4)]
-        acc = [[None] * 2 for m in range(4)]
-
-        def sort_half(m, s):
-            ordered[m][s] = keep.tile([P, 4, 2, P], F32, name="ordered_%d_%d" % (m, s))
+        def sort_piece(m, i):
+            n = len(pieces[m][i])
+            ordered[(m, i)] = keep.tile([P, 2 * n, 2, P], F32, name="ordered_%d_%d" % (m, i))
             nc.vector.tensor_copy(
-                out=ordered[m][s][:],
-                in_=x_sb[m][s][:].bitcast(F32).rearrange("p (g j u) -> p g u j", j=P, u=2),
+                out=ordered[(m, i)][:],
+                in_=x_sb[(m, i)][:].bitcast(F32).rearrange("p (g j u) -> p g u j", j=P, u=2),
             )
 
-        def transpose_half(m, s, first_bank):
-            words = x_sb[m][s][:].bitcast(F32)
-            for jj in range(2):
-                j = 2 * s + jj
-                bank = psum.tile([P, 2, 2, P], F32, tag="t%d" % (first_bank + jj), name="xt_%d_%d" % (m, j))
-                for gg in range(2):
-                    for u in range(2):
-                        c0 = 256 * (2 * jj + gg)
-                        if ordered[m][s] is None:
-                            nc.tensor.transpose(bank[:, gg, u, :], words[:, c0 + u : c0 + 256 : 2], ident[:])
-                        else:
-                            nc.tensor.transpose(bank[:, gg, u, :], ordered[m][s][:, 2 * jj + gg, u, :], ident[:])
-                grouped[m][j] = keep.tile([P, 2, P, 4], BF16, name="grouped_%d_%d" % (m, j), align_bytes=64)
-                nc.scalar.copy(out=grouped[m][j][:].bitcast(F32), in_=bank[:].rearrange("p g u r -> p g r u"))
+        def transposes(m, j, bank):
+            i, jj = where[(m, j)]
+            banks[(m, j)] = psum.tile([P, 2, 2, P], F32, tag="t%d" % bank, name="xt_%d_%d" % (m, j))
+            words = x_sb[(m, i)][:].bitcast(F32)
+            for gg in range(2):
+                for u in range(2):
+                    c0 = 256 * (2 * jj + gg)
+                    if (m, i) in ordered:
+                        nc.tensor.transpose(banks[(m, j)][:, gg, u, :], ordered[(m, i)][:, 2 * jj + gg, u, :], ident[:])
+                    else:
+                        nc.tensor.transpose(banks[(m, j)][:, gg, u, :], words[:, c0 + u : c0 + 256 : 2], ident[:])
+
+        def copy_out(m, j, engine):
+            grouped[(m, j)] = keep.tile([P, 2, P, 4], BF16, name="grouped_%d_%d" % (m, j), align_bytes=64)
+            source = banks[(m, j)][:].rearrange("p g u r -> p g r u")
+            if engine == 0:
+                nc.scalar.copy(out=grouped[(m, j)][:].bitcast(F32), in_=source)
+            else:
+                nc.vector.tensor_copy(out=grouped[(m, j)][:].bitcast(F32), in_=source)
 
         def quantise(m, j):
-            codes[m][j] = keep.tile([P, 2, P], U32, name="codes_%d_%d" % (m, j), align_bytes=64)
-            x_planes[m][j] = keep.tile([P, 2, P], U8, name="x_planes_%d_%d" % (m, j), align_bytes=64)
+            codes[(m, j)] = keep.tile([P, 2, P], U32, name="codes_%d_%d" % (m, j), align_bytes=64)
+            x_planes[(m, j)] = keep.tile([P, 2, P], U8, name="x_planes_%d_%d" % (m, j), align_bytes=64)
             nc.vector.quantize_mx(
-                out=codes[m][j][:].rearrange("p g r -> p (g r)").bitcast(FP8X4),
-                scales=x_planes[m][j][:].rearrange("p g r -> p (g r)"),
-                in_=grouped[m][j][:].rearrange("p g r t -> p (g r t)"),
+                out=codes[(m, j)][:].rearrange("p g r -> p (g r)").bitcast(FP8X4),
+                scales=x_planes[(m, j)][:].rearrange("p g r -> p (g r)"),
+                in_=grouped[(m, j)][:].rearrange("p g r t -> p (g r t)"),
             )
 
-        def mx_pass(m, h, g):
-            if g == 0:
-                acc[m][h] = psum.tile([P, NH], F32, tag="a%d" % (2 * (m % 2) + h), name="acc_%d_%d" % (m, h))
+        def mx_pass(m, h, g, c0, c1):
+            if g == 0 and c0 == 0:
+                acc[(m, h)] = psum.tile([P, NH], F32, tag="a%d" % (2 * (m % 2) + h), name="acc_%d_%d" % (m, h))
+            s, gl = plane_of[g]
             nc.tensor.matmul_mx(
-                out=acc[m][h][:],
-                lhsT=codes[m][g // 2][:, g % 2, :].bitcast(FP8X4),
-                lhsT_scale=x_planes[m][g // 2][:, g % 2, :],
-                rhs=w_words[g][:, 2 * NH * h : 2 * NH * (h + 1)].bitcast(FP4X4),
-                rhs_scale=planes[g // 4][:, g % 4, NH * h : NH * (h + 1)],
+                out=acc[(m, h)][:, c0:c1],
+                lhsT=codes[(m, g // 2)][:, g % 2, :].bitcast(FP8X4),
+                lhsT_scale=x_planes[(m, g // 2)][:, g % 2, :],
+                rhs=w_words[g][:, 2 * (NH * h + c0) : 2 * (NH * h + c1)].bitcast(FP4X4),
+                rhs_scale=planes[s][:, gl, NH * h + c0 : NH * h + c1],
                 start=(g == 0),
                 stop=(g == 7),
             )
 
-        def finish(m, h):
-            result = keep.tile([P, NH], F32, name="result_%d_%d" % (m, h))
-            nc.vector.tensor_tensor(out=result[:], in0=acc[m][h][:], in1=bias_all[:, NH * h : NH * (h + 1)], op=ADD)
-            nc.sync.dma_start(out=y[P * m : P * (m + 1), NH * h : NH * (h + 1)], in_=result[:])
+        def mx_pass_narrow(m, h, g, c, bank):
+            if g == 0:
+                acc[(m, h, c)] = psum.tile([P, P], F32, tag="t%d" % bank, name="acc_%d_%d_%d" % (m, h, c))
+            s, gl = plane_of[g]
+            c0 = NH * h + P * c
+            nc.tensor.matmul_mx(
+                out=acc[(m, h, c)][:],
+                lhsT=codes[(m, g // 2)][:, g % 2, :].bitcast(FP8X4),
+                lhsT_scale=x_planes[(m, g // 2)][:, g % 2, :],
+                rhs=w_words[g][:, 2 * c0 : 2 * (c0 + P)].bitcast(FP4X4),
+                rhs_scale=planes[s][:, gl, c0 : c0 + P],
+                start=(g == 0),
+                stop=(g == 7),
+            )
 
-        def group(m, h, first, last):
-            for g in range(first, last):
-                mx_pass(m, h, g)
-            if last == 8:
-                finish(m, h)
+        def finish_narrow(m, h, c, queue):
+            c0 = NH * h + P * c
+            narrow = keep.tile([P, P], F32, name="narrow_%d_%d_%d" % (m, h, c))
+            nc.vector.tensor_tensor(out=narrow[:], in0=acc[(m, h, c)][:], in1=bias_all[:, c0 : c0 + P], op=ADD)
+            queue.dma_start(out=y[P * m : P * (m + 1), c0 : c0 + P], in_=narrow[:])
 
-        transpose_half(0, 0, 0)
-        quantise(0, 0)
-        quantise(0, 1)
-        transpose_half(1, 0, 2)
-        quantise(1, 0)
-        quantise(1, 1)
-        for g in range(4):
-            for m in (0, 1):
-                for h in range(2):
-                    mx_pass(m, h, g)
-        sort_half(0, 1)
-        sort_half(1, 1)
-        for h in range(2):
-            spread = psum.tile([P, NH], F32, tag="t%d" % h, name="spread_%d" % h)
+        def add_bias(m, h, c0, c1):
+            result[(m, h, c0)] = keep.tile([P, c1 - c0], F32, name="result_%d_%d_%d" % (m, h, c0))
+            nc.vector.tensor_tensor(
+                out=result[(m, h, c0)][:], in0=acc[(m, h)][:, c0:c1], in1=bias_all[:, NH * h + c0 : NH * h + c1], op=ADD
+            )
+
+        def store(m, h, c0, c1, queue):
+            queue.dma_start(out=y[P * m : P * (m + 1), NH * h + c0 : NH * h + c1], in_=result[(m, h, c0)][:])
+
+        def spread_bias(h, bank, engine):
+            spread = psum.tile([P, NH], F32, tag="t%d" % bank, name="spread_%d" % h)
             nc.tensor.matmul(out=spread[:], lhsT=ones[:], rhs=bias_row[:, NH * h : NH * (h + 1)], start=True, stop=True)
-            if h == 0:
-                nc.scalar.copy(out=bias_all[:, 0:NH], in_=spread[:])
+            if engine == 0:
+                nc.scalar.copy(out=bias_all[:, NH * h : NH * (h + 1)], in_=spread[:])
             else:
-                nc.vector.tensor_copy(out=bias_all[:, NH : 2 * NH], in_=spread[:])
-        transpose_half(0, 1, 2)
+                nc.vector.tensor_copy(out=bias_all[:, NH * h : NH * (h + 1)], in_=spread[:])
+
+        nc.vector.memset(bias_row[:], 0.0)
+        zero_planes(0)
+        zero_planes(1)
+        zero_planes(2)
+        nc.vector.memset(ones[:], 1.0)
+        make_identity(nc, ident[:])
+        nc.scalar.dma_start(out=bias_row[0:1, :], in_=bias.rearrange("(o n) -> o n", o=1))
+        load_x(0, 0, nc.sync)
+        load_x(1, 0, nc.sync)
+        load_scales(0, nc.sync, I32)
+        load_w(0)
+        load_scales(2, nc.gpsimd, F32)
+        load_x(0, 1, nc.sync)
+        load_x(1, 1, nc.sync)
+        load_w(1)
+        load_scales(1, nc.sync, I32)
+        load_w(2)
+        load_w(3)
+        load_x(0, 2, nc.sync)
+        load_x(1, 2, nc.sync)
+        load_w(4)
+        load_w(5)
+        load_w(6)
+        load_w(7)
+        load_x(2, 0, nc.sync)
+        load_x(2, 1, nc.sync)
+        load_x(3, 0, nc.sync)
+        load_x(3, 1, nc.sync)
+        transposes(0, 0, 0)
+        copy_out(0, 0, 0)
+        quantise(0, 0)
+        transposes(1, 0, 1)
+        copy_out(1, 0, 0)
+        quantise(1, 0)
+        mx_pass(0, 0, 0, 0, 512)
+        mx_pass(0, 1, 0, 0, 512)
+        mx_pass(1, 0, 0, 0, 512)
+        mx_pass(1, 1, 0, 0, 512)
+        transposes(0, 1, 2)
+        copy_out(0, 1, 0)
+        quantise(0, 1)
+        transposes(1, 1, 3)
+        copy_out(1, 1, 0)
+        quantise(1, 1)
+        mx_pass(0, 0, 1, 0, 512)
+        mx_pass(0, 1, 1, 0, 512)
+        mx_pass(1, 0, 1, 0, 512)
+        mx_pass(1, 1, 1, 0, 512)
+        mx_pass(0, 0, 2, 0, 512)
+        mx_pass(0, 1, 2, 0, 512)
+        mx_pass(1, 0, 2, 0, 512)
+        mx_pass(1, 1, 2, 0, 512)
+        mx_pass(0, 0, 3, 0, 512)
+        mx_pass(0, 1, 3, 0, 512)
+        mx_pass(1, 0, 3, 0, 512)
+        mx_pass(1, 1, 3, 0, 512)
+        sort_piece(0, 2)
+        sort_piece(1, 2)
+        transposes(0, 2, 0)
+        copy_out(0, 2, 0)
+        transposes(0, 3, 1)
+        copy_out(0, 3, 0)
         quantise(0, 2)
         quantise(0, 3)
-        transpose_half(1, 1, 0)
+        transposes(1, 2, 2)
+        copy_out(1, 2, 0)
+        transposes(1, 3, 3)
+        copy_out(1, 3, 0)
         quantise(1, 2)
         quantise(1, 3)
-        group(0, 0, 4, 8)
-        group(0, 1, 4, 8)
-        sort_half(2, 0)
-        group(1, 0, 4, 8)
-        sort_half(2, 1)
-        group(1, 1, 4, 8)
-        sort_half(3, 0)
-        transpose_half(2, 0, 2)
-        transpose_half(2, 1, 0)
-        transpose_half(3, 0, 2)
-        for j in range(4):
-            quantise(2, j)
-        sort_half(3, 1)
+        spread_bias(0, 0, 0)
+        spread_bias(1, 1, 1)
+        mx_pass(0, 0, 4, 0, 512)
+        mx_pass(0, 1, 4, 0, 512)
+        mx_pass(0, 0, 5, 0, 512)
+        mx_pass(0, 1, 5, 0, 512)
+        mx_pass(0, 0, 6, 0, 512)
+        mx_pass(0, 1, 6, 0, 512)
+        mx_pass(0, 0, 7, 0, 512)
+        mx_pass(0, 1, 7, 0, 512)
+        sort_piece(2, 0)
+        add_bias(0, 0, 0, 512)
+        store(0, 0, 0, 512, nc.sync)
+        add_bias(0, 1, 0, 512)
+        store(0, 1, 0, 512, nc.sync)
+        sort_piece(2, 1)
+        mx_pass(1, 0, 4, 0, 512)
+        mx_pass(1, 1, 4, 0, 512)
+        mx_pass(1, 0, 5, 0, 512)
+        mx_pass(1, 1, 5, 0, 512)
+        mx_pass(1, 0, 6, 0, 512)
+        mx_pass(1, 1, 6, 0, 512)
+        transposes(2, 0, 2)
+        copy_out(2, 0, 0)
+        transposes(2, 1, 3)
+        copy_out(2, 1, 0)
+        transposes(2, 2, 0)
+        copy_out(2, 2, 0)
+        transposes(2, 3, 1)
+        copy_out(2, 3, 0)
+        quantise(2, 0)
+        quantise(2, 1)
+        mx_pass(1, 0, 7, 0, 512)
+        mx_pass(1, 1, 7, 0, 512)
+        quantise(2, 2)
+        quantise(2, 3)
+        sort_piece(3, 0)
+        add_bias(1, 0, 0, 512)
+        store(1, 0, 0, 512, nc.sync)
+        sort_piece(3, 1)
+        add_bias(1, 1, 0, 512)
+        store(1, 1, 0, 512, nc.sync)
+        mx_pass(2, 0, 0, 0, 512)
+        mx_pass(2, 0, 1, 0, 512)
+        mx_pass(2, 0, 2, 0, 512)
+        mx_pass(2, 0, 3, 0, 512)
+        mx_pass(2, 0, 4, 0, 512)
+        mx_pass(2, 0, 5, 0, 512)
+        mx_pass(2, 0, 6, 0, 512)
+        mx_pass(2, 0, 7, 0, 512)
+        add_bias(2, 0, 0, 512)
+        store(2, 0, 0, 512, nc.sync)
+        transposes(3, 0, 2)
+        copy_out(3, 0, 0)
+        transposes(3, 1, 3)
+        copy_out(3, 1, 0)
+        transposes(3, 2, 0)
+        copy_out(3, 2, 0)
+        transposes(3, 3, 1)
+        copy_out(3, 3, 0)
         quantise(3, 0)
         quantise(3, 1)
-        group(2, 0, 0, 8)
-        transpose_half(3, 1, 0)
         quantise(3, 2)
         quantise(3, 3)
-        group(2, 1, 0, 8)
-        group(3, 0, 0, 8)
-        group(3, 1, 0, 8)
+        mx_pass(2, 1, 0, 0, 512)
+        mx_pass(2, 1, 1, 0, 512)
+        mx_pass(2, 1, 2, 0, 512)
+        mx_pass(2, 1, 3, 0, 512)
+        mx_pass(2, 1, 4, 0, 512)
+        mx_pass(2, 1, 5, 0, 512)
+        mx_pass(2, 1, 6, 0, 512)
+        mx_pass(2, 1, 7, 0, 512)
+        add_bias(2, 1, 0, 512)
+        store(2, 1, 0, 512, nc.sync)
+        mx_pass(3, 0, 0, 0, 512)
+        mx_pass(3, 0, 1, 0, 512)
+        mx_pass(3, 0, 2, 0, 512)
+        mx_pass(3, 0, 3, 0, 512)
+        mx_pass(3, 0, 4, 0, 512)
+        mx_pass(3, 0, 5, 0, 512)
+        mx_pass(3, 0, 6, 0, 512)
+        mx_pass(3, 0, 7, 0, 512)
+        add_bias(3, 0, 0, 512)
+        store(3, 0, 0, 512, nc.sync)
+        mx_pass_narrow(3, 1, 0, 0, 0)
+        mx_pass_narrow(3, 1, 1, 0, 0)
+        mx_pass_narrow(3, 1, 2, 0, 0)
+        mx_pass_narrow(3, 1, 3, 0, 0)
+        mx_pass_narrow(3, 1, 4, 0, 0)
+        mx_pass_narrow(3, 1, 5, 0, 0)
+        mx_pass_narrow(3, 1, 6, 0, 0)
+        mx_pass_narrow(3, 1, 7, 0, 0)
+        finish_narrow(3, 1, 0, nc.sync)
+        mx_pass_narrow(3, 1, 0, 1, 1)
+        mx_pass_narrow(3, 1, 1, 1, 1)
+        mx_pass_narrow(3, 1, 2, 1, 1)
+        mx_pass_narrow(3, 1, 3, 1, 1)
+        mx_pass_narrow(3, 1, 4, 1, 1)
+        mx_pass_narrow(3, 1, 5, 1, 1)
+        mx_pass_narrow(3, 1, 6, 1, 1)
+        mx_pass_narrow(3, 1, 7, 1, 1)
+        finish_narrow(3, 1, 1, nc.sync)
+        mx_pass_narrow(3, 1, 0, 2, 2)
+        mx_pass_narrow(3, 1, 1, 2, 2)
+        mx_pass_narrow(3, 1, 2, 2, 2)
+        mx_pass_narrow(3, 1, 3, 2, 2)
+        mx_pass_narrow(3, 1, 4, 2, 2)
+        mx_pass_narrow(3, 1, 5, 2, 2)
+        mx_pass_narrow(3, 1, 6, 2, 2)
+        mx_pass_narrow(3, 1, 7, 2, 2)
+        finish_narrow(3, 1, 2, nc.sync)
+        mx_pass_narrow(3, 1, 0, 3, 3)
+        mx_pass_narrow(3, 1, 1, 3, 3)
+        mx_pass_narrow(3, 1, 2, 3, 3)
+        mx_pass_narrow(3, 1, 3, 3, 3)
+        mx_pass_narrow(3, 1, 4, 3, 3)
+        mx_pass_narrow(3, 1, 5, 3, 3)
+        mx_pass_narrow(3, 1, 6, 3, 3)
+        mx_pass_narrow(3, 1, 7, 3, 3)
+        finish_narrow(3, 1, 3, nc.sync)

@@ -174,7 +174,6 @@ def tile_terowparallellinear_kernel(tc, input_, weight_words, weight_scales, bia
         load_x(1, 0, nc.sync)
         load_scales(0, nc.sync, I32)
         load_w(0)
-        load_scales(2, nc.gpsimd, F32)
         load_x(0, 1, nc.sync)
         load_x(1, 1, nc.sync)
         load_w(1)
@@ -183,12 +182,13 @@ def tile_terowparallellinear_kernel(tc, input_, weight_words, weight_scales, bia
         load_w(3)
         load_x(0, 2, nc.sync)
         load_x(1, 2, nc.sync)
+        load_scales(2, nc.sync, I32)
         load_w(4)
         load_w(5)
         load_w(6)
-        load_w(7)
         load_x(2, 0, nc.sync)
         load_x(2, 1, nc.sync)
+        load_w(7)
         load_x(3, 0, nc.sync)
         load_x(3, 1, nc.sync)
         transposes(0, 0, 0)
@@ -224,7 +224,7 @@ def tile_terowparallellinear_kernel(tc, input_, weight_words, weight_scales, bia
         transposes(0, 2, 0)
         copy_out(0, 2, 0)
         transposes(0, 3, 1)
-        copy_out(0, 3, 0)
+        copy_out(0, 3, 1)
         quantise(0, 2)
         quantise(0, 3)
         transposes(1, 2, 2)
@@ -237,24 +237,18 @@ def tile_terowparallellinear_kernel(tc, input_, weight_words, weight_scales, bia
         spread_bias(1, 1, 1)
         mx_pass(0, 0, 4, 0, 512)
         mx_pass(0, 1, 4, 0, 512)
-        mx_pass(0, 0, 5, 0, 512)
-        mx_pass(0, 1, 5, 0, 512)
-        mx_pass(0, 0, 6, 0, 512)
-        mx_pass(0, 1, 6, 0, 512)
-        mx_pass(0, 0, 7, 0, 512)
-        mx_pass(0, 1, 7, 0, 512)
-        sort_piece(2, 0)
-        add_bias(0, 0, 0, 512)
-        store(0, 0, 0, 512, nc.sync)
-        add_bias(0, 1, 0, 512)
-        store(0, 1, 0, 512, nc.sync)
-        sort_piece(2, 1)
         mx_pass(1, 0, 4, 0, 512)
         mx_pass(1, 1, 4, 0, 512)
+        mx_pass(0, 0, 5, 0, 512)
+        mx_pass(0, 1, 5, 0, 512)
         mx_pass(1, 0, 5, 0, 512)
         mx_pass(1, 1, 5, 0, 512)
+        mx_pass(0, 0, 6, 0, 512)
+        mx_pass(0, 1, 6, 0, 512)
         mx_pass(1, 0, 6, 0, 512)
         mx_pass(1, 1, 6, 0, 512)
+        sort_piece(2, 0)
+        sort_piece(2, 1)
         transposes(2, 0, 2)
         copy_out(2, 0, 0)
         transposes(2, 1, 3)
@@ -265,14 +259,20 @@ def tile_terowparallellinear_kernel(tc, input_, weight_words, weight_scales, bia
         copy_out(2, 3, 0)
         quantise(2, 0)
         quantise(2, 1)
+        mx_pass(0, 0, 7, 0, 512)
+        mx_pass(0, 1, 7, 0, 512)
         mx_pass(1, 0, 7, 0, 512)
         mx_pass(1, 1, 7, 0, 512)
+        add_bias(0, 0, 0, 512)
+        store(0, 0, 0, 512, nc.sync)
+        add_bias(0, 1, 0, 512)
+        store(0, 1, 0, 512, nc.sync)
         quantise(2, 2)
         quantise(2, 3)
         sort_piece(3, 0)
+        sort_piece(3, 1)
         add_bias(1, 0, 0, 512)
         store(1, 0, 0, 512, nc.sync)
-        sort_piece(3, 1)
         add_bias(1, 1, 0, 512)
         store(1, 1, 0, 512, nc.sync)
         mx_pass(2, 0, 0, 0, 512)

@@ -29,7 +29,7 @@ def tile_terowparallellinear_kernel(tc, input_, weight_words, weight_scales, bia
     with ExitStack() as ctx:
         keep = ctx.enter_context(tc.tile_pool(name="keep", bufs=1))
         psum = ctx.enter_context(tc.psum_pool(name="psum", bufs=1))
-        ctx.enter_context(tc.manual_schedule())
+
 
         pieces = [[[0],[1],[2,3]],[[0],[1],[2,3]],[[0,1],[2,3]],[[0,1],[2,3]]]
         plane_groups = [[0,2],[2,4],[4,8]]
@@ -48,7 +48,12 @@ def tile_terowparallellinear_kernel(tc, input_, weight_words, weight_scales, bia
         bias_all = keep.tile([P, N], F32, name="bias_all")
         ones = keep.tile([P, P], BF16, name="ones")
         ident = keep.tile([P, P], F32, name="ident")
-        w_words = [keep.tile([P, 2 * N], U8, name="w_words_%d" % g, align_bytes=64) for g in range(8)]
+        w_groups = [[0],[1],[2],[3],[4],[5],[6],[7]]
+        w_tiles = [keep.tile([P, len(gs), 2 * N], U8, name="w_words_%d" % gs[0], align_bytes=64) for gs in w_groups]
+        w_words = {}
+        for t in range(len(w_groups)):
+            for gl in range(len(w_groups[t])):
+                w_words[w_groups[t][gl]] = w_tiles[t][:, gl, :]
         x_sb = {}
         ordered = {}
         banks = {}
@@ -66,8 +71,23 @@ def tile_terowparallellinear_kernel(tc, input_, weight_words, weight_scales, bia
             x_sb[(m, i)] = keep.tile([P, 1024 * len(js)], BF16, name="x_%d_%d" % (m, i))
             queue.dma_start(out=x_sb[(m, i)][:], in_=x[P * m : P * (m + 1), 1024 * js[0] : 1024 * (js[-1] + 1)])
 
-        def load_w(g):
-            nc.sync.dma_start(out=w_words[g][:].bitcast(I32), in_=weight_words[g].bitcast(I32))
+        def load_x_pair(m, i, queue):
+            js = pieces[m][i]
+            width = 1024 * len(js)
+            pair = keep.tile([P, 2, width], BF16, name="xpair_%d_%d" % (m, i))
+            queue.dma_start(
+                out=pair[:],
+                in_=x[P * m : P * (m + 2), 1024 * js[0] : 1024 * (js[-1] + 1)].rearrange("(m p) k -> p m k", p=P),
+            )
+            x_sb[(m, i)] = pair[:, 0, :]
+            x_sb[(m + 1, i)] = pair[:, 1, :]
+
+        def load_w(t):
+            gs = w_groups[t]
+            nc.sync.dma_start(
+                out=w_tiles[t][:].bitcast(I32),
+                in_=weight_words[gs[0] : gs[-1] + 1].rearrange("g p n -> p g n").bitcast(I32),
+            )
 
         def load_scales(s, queue, view):
             g0, g1 = plane_groups[s]
@@ -84,7 +104,7 @@ def tile_terowparallellinear_kernel(tc, input_, weight_words, weight_scales, bia
 
         def transposes(m, j, bank):
             i, jj = where[(m, j)]
-            banks[(m, j)] = psum.tile([P, 2, 2, P], F32, tag="t%d" % bank, name="xt_%d_%d" % (m, j))
+            banks[(m, j)] = psum.tile([P, 2, 2, P], F32, tag=bank, name="xt_%d_%d" % (m, j))
             words = x_sb[(m, i)][:].bitcast(F32)
             for gg in range(2):
                 for u in range(2):
@@ -127,7 +147,7 @@ def tile_terowparallellinear_kernel(tc, input_, weight_words, weight_scales, bia
 
         def mx_pass_narrow(m, h, g, c, bank):
             if g == 0:
-                acc[(m, h, c)] = psum.tile([P, P], F32, tag="t%d" % bank, name="acc_%d_%d_%d" % (m, h, c))
+                acc[(m, h, c)] = psum.tile([P, P], F32, tag=bank, name="acc_%d_%d_%d" % (m, h, c))
             s, gl = plane_of[g]
             c0 = NH * h + P * c
             nc.tensor.matmul_mx(
@@ -156,7 +176,7 @@ def tile_terowparallellinear_kernel(tc, input_, weight_words, weight_scales, bia
             queue.dma_start(out=y[P * m : P * (m + 1), NH * h + c0 : NH * h + c1], in_=result[(m, h, c0)][:])
 
         def spread_bias(h, bank, engine):
-            spread = psum.tile([P, NH], F32, tag="t%d" % bank, name="spread_%d" % h)
+            spread = psum.tile([P, NH], F32, tag=bank, name="spread_%d" % h)
             nc.tensor.matmul(out=spread[:], lhsT=ones[:], rhs=bias_row[:, NH * h : NH * (h + 1)], start=True, stop=True)
             if engine == 0:
                 nc.scalar.copy(out=bias_all[:, NH * h : NH * (h + 1)], in_=spread[:])
@@ -191,20 +211,20 @@ def tile_terowparallellinear_kernel(tc, input_, weight_words, weight_scales, bia
         load_w(7)
         load_x(3, 0, nc.sync)
         load_x(3, 1, nc.sync)
-        transposes(0, 0, 0)
+        transposes(0, 0, "t0")
         copy_out(0, 0, 0)
         quantise(0, 0)
-        transposes(1, 0, 1)
+        transposes(1, 0, "t1")
         copy_out(1, 0, 0)
         quantise(1, 0)
         mx_pass(0, 0, 0, 0, 512)
         mx_pass(0, 1, 0, 0, 512)
         mx_pass(1, 0, 0, 0, 512)
         mx_pass(1, 1, 0, 0, 512)
-        transposes(0, 1, 2)
+        transposes(0, 1, "t2")
         copy_out(0, 1, 0)
         quantise(0, 1)
-        transposes(1, 1, 3)
+        transposes(1, 1, "t3")
         copy_out(1, 1, 0)
         quantise(1, 1)
         mx_pass(0, 0, 1, 0, 512)
@@ -221,20 +241,20 @@ def tile_terowparallellinear_kernel(tc, input_, weight_words, weight_scales, bia
         mx_pass(1, 1, 3, 0, 512)
         sort_piece(0, 2)
         sort_piece(1, 2)
-        transposes(0, 2, 0)
+        transposes(0, 2, "t0")
         copy_out(0, 2, 0)
-        transposes(0, 3, 1)
+        transposes(0, 3, "t1")
         copy_out(0, 3, 1)
         quantise(0, 2)
         quantise(0, 3)
-        transposes(1, 2, 2)
+        transposes(1, 2, "t2")
         copy_out(1, 2, 0)
-        transposes(1, 3, 3)
+        transposes(1, 3, "t3")
         copy_out(1, 3, 0)
         quantise(1, 2)
         quantise(1, 3)
-        spread_bias(0, 0, 0)
-        spread_bias(1, 1, 1)
+        spread_bias(0, "t0", 0)
+        spread_bias(1, "t1", 1)
         mx_pass(0, 0, 4, 0, 512)
         mx_pass(0, 1, 4, 0, 512)
         mx_pass(1, 0, 4, 0, 512)
@@ -249,13 +269,13 @@ def tile_terowparallellinear_kernel(tc, input_, weight_words, weight_scales, bia
         mx_pass(1, 1, 6, 0, 512)
         sort_piece(2, 0)
         sort_piece(2, 1)
-        transposes(2, 0, 2)
+        transposes(2, 0, "t2")
         copy_out(2, 0, 0)
-        transposes(2, 1, 3)
+        transposes(2, 1, "t3")
         copy_out(2, 1, 0)
-        transposes(2, 2, 0)
+        transposes(2, 2, "t0")
         copy_out(2, 2, 0)
-        transposes(2, 3, 1)
+        transposes(2, 3, "t1")
         copy_out(2, 3, 0)
         quantise(2, 0)
         quantise(2, 1)
@@ -285,13 +305,13 @@ def tile_terowparallellinear_kernel(tc, input_, weight_words, weight_scales, bia
         mx_pass(2, 0, 7, 0, 512)
         add_bias(2, 0, 0, 512)
         store(2, 0, 0, 512, nc.sync)
-        transposes(3, 0, 2)
+        transposes(3, 0, "t2")
         copy_out(3, 0, 0)
-        transposes(3, 1, 3)
+        transposes(3, 1, "t3")
         copy_out(3, 1, 0)
-        transposes(3, 2, 0)
+        transposes(3, 2, "t0")
         copy_out(3, 2, 0)
-        transposes(3, 3, 1)
+        transposes(3, 3, "t1")
         copy_out(3, 3, 0)
         quantise(3, 0)
         quantise(3, 1)
@@ -317,39 +337,39 @@ def tile_terowparallellinear_kernel(tc, input_, weight_words, weight_scales, bia
         mx_pass(3, 0, 7, 0, 512)
         add_bias(3, 0, 0, 512)
         store(3, 0, 0, 512, nc.sync)
-        mx_pass_narrow(3, 1, 0, 0, 0)
-        mx_pass_narrow(3, 1, 1, 0, 0)
-        mx_pass_narrow(3, 1, 2, 0, 0)
-        mx_pass_narrow(3, 1, 3, 0, 0)
-        mx_pass_narrow(3, 1, 4, 0, 0)
-        mx_pass_narrow(3, 1, 5, 0, 0)
-        mx_pass_narrow(3, 1, 6, 0, 0)
-        mx_pass_narrow(3, 1, 7, 0, 0)
+        mx_pass_narrow(3, 1, 0, 0, "t0")
+        mx_pass_narrow(3, 1, 1, 0, "t0")
+        mx_pass_narrow(3, 1, 2, 0, "t0")
+        mx_pass_narrow(3, 1, 3, 0, "t0")
+        mx_pass_narrow(3, 1, 4, 0, "t0")
+        mx_pass_narrow(3, 1, 5, 0, "t0")
+        mx_pass_narrow(3, 1, 6, 0, "t0")
+        mx_pass_narrow(3, 1, 7, 0, "t0")
         finish_narrow(3, 1, 0, nc.sync)
-        mx_pass_narrow(3, 1, 0, 1, 1)
-        mx_pass_narrow(3, 1, 1, 1, 1)
-        mx_pass_narrow(3, 1, 2, 1, 1)
-        mx_pass_narrow(3, 1, 3, 1, 1)
-        mx_pass_narrow(3, 1, 4, 1, 1)
-        mx_pass_narrow(3, 1, 5, 1, 1)
-        mx_pass_narrow(3, 1, 6, 1, 1)
-        mx_pass_narrow(3, 1, 7, 1, 1)
+        mx_pass_narrow(3, 1, 0, 1, "t1")
+        mx_pass_narrow(3, 1, 1, 1, "t1")
+        mx_pass_narrow(3, 1, 2, 1, "t1")
+        mx_pass_narrow(3, 1, 3, 1, "t1")
+        mx_pass_narrow(3, 1, 4, 1, "t1")
+        mx_pass_narrow(3, 1, 5, 1, "t1")
+        mx_pass_narrow(3, 1, 6, 1, "t1")
+        mx_pass_narrow(3, 1, 7, 1, "t1")
         finish_narrow(3, 1, 1, nc.sync)
-        mx_pass_narrow(3, 1, 0, 2, 2)
-        mx_pass_narrow(3, 1, 1, 2, 2)
-        mx_pass_narrow(3, 1, 2, 2, 2)
-        mx_pass_narrow(3, 1, 3, 2, 2)
-        mx_pass_narrow(3, 1, 4, 2, 2)
-        mx_pass_narrow(3, 1, 5, 2, 2)
-        mx_pass_narrow(3, 1, 6, 2, 2)
-        mx_pass_narrow(3, 1, 7, 2, 2)
+        mx_pass_narrow(3, 1, 0, 2, "t2")
+        mx_pass_narrow(3, 1, 1, 2, "t2")
+        mx_pass_narrow(3, 1, 2, 2, "t2")
+        mx_pass_narrow(3, 1, 3, 2, "t2")
+        mx_pass_narrow(3, 1, 4, 2, "t2")
+        mx_pass_narrow(3, 1, 5, 2, "t2")
+        mx_pass_narrow(3, 1, 6, 2, "t2")
+        mx_pass_narrow(3, 1, 7, 2, "t2")
         finish_narrow(3, 1, 2, nc.sync)
-        mx_pass_narrow(3, 1, 0, 3, 3)
-        mx_pass_narrow(3, 1, 1, 3, 3)
-        mx_pass_narrow(3, 1, 2, 3, 3)
-        mx_pass_narrow(3, 1, 3, 3, 3)
-        mx_pass_narrow(3, 1, 4, 3, 3)
-        mx_pass_narrow(3, 1, 5, 3, 3)
-        mx_pass_narrow(3, 1, 6, 3, 3)
-        mx_pass_narrow(3, 1, 7, 3, 3)
+        mx_pass_narrow(3, 1, 0, 3, "t3")
+        mx_pass_narrow(3, 1, 1, 3, "t3")
+        mx_pass_narrow(3, 1, 2, 3, "t3")
+        mx_pass_narrow(3, 1, 3, 3, "t3")
+        mx_pass_narrow(3, 1, 4, 3, "t3")
+        mx_pass_narrow(3, 1, 5, 3, "t3")
+        mx_pass_narrow(3, 1, 6, 3, "t3")
+        mx_pass_narrow(3, 1, 7, 3, "t3")
         finish_narrow(3, 1, 3, nc.sync)

from contextlib import ExitStack

import concourse.mybir as mybir
from concourse.masks import make_identity

F32 = mybir.dt.float32
BF16 = mybir.dt.bfloat16
U8 = mybir.dt.uint8
U32 = mybir.dt.uint32
I32 = mybir.dt.int32
FP8X4 = mybir.dt.float8_e4m3fn_x4
FP4X4 = mybir.dt.float4_e2m1fn_x4
ADD = mybir.AluOpType.add

P = 128
TOKENS = 512
K = 4096
N = 1024
NH = 512
FLOPS = 2 * TOKENS * K * N


def tile_terowparallellinear_kernel(tc, input_, weight_words, weight_scales, bias, out):
    nc = tc.nc
    x = input_.flatten_outer_dims()
    y = out.flatten_outer_dims()
    scale_rows = weight_scales.rearrange("g q n -> q g n")

    with ExitStack() as ctx:
        keep = ctx.enter_context(tc.tile_pool(name="keep", bufs=1))
        psum = ctx.enter_context(tc.psum_pool(name="psum", bufs=1))


        pieces = [[[0],[1],[2,3]],[[0],[1],[2,3]],[[0,1],[2,3]],[[0,1],[2,3]]]
        plane_groups = [[0,2],[2,4],[4,8]]
        where = {}
        for m in range(4):
            for i in range(len(pieces[m])):
                for jj in range(len(pieces[m][i])):
                    where[(m, pieces[m][i][jj])] = (i, jj)
        plane_of = {}
        for s in range(len(plane_groups)):
            for g in range(plane_groups[s][0], plane_groups[s][1]):
                plane_of[g] = (s, g - plane_groups[s][0])

        planes = [keep.tile([P, r[1] - r[0], N], U8, name="w_planes_%d" % r[0], align_bytes=64) for r in plane_groups]
        bias_row = keep.tile([P, N], BF16, name="bias_row")
        bias_all = keep.tile([P, N], F32, name="bias_all")
        ones = keep.tile([P, P], BF16, name="ones")
        ident = keep.tile([P, P], F32, name="ident")
        w_groups = [[0],[1],[2],[3],[4],[5],[6],[7]]
        w_tiles = [keep.tile([P, len(gs), 2 * N], U8, name="w_words_%d" % gs[0], align_bytes=64) for gs in w_groups]
        w_words = {}
        for t in range(len(w_groups)):
            for gl in range(len(w_groups[t])):
                w_words[w_groups[t][gl]] = w_tiles[t][:, gl, :]
        x_sb = {}
        ordered = {}
        banks = {}
        grouped = {}
        codes = {}
        x_planes = {}
        acc = {}
        result = {}

        def zero_planes(s):
            nc.vector.memset(planes[s][:].rearrange("p g n -> p (g n)").bitcast(I32), 0)

        def load_x(m, i, queue):
            js = pieces[m][i]
            x_sb[(m, i)] = keep.tile([P, 1024 * len(js)], BF16, name="x_%d_%d" % (m, i))
            queue.dma_start(out=x_sb[(m, i)][:], in_=x[P * m : P * (m + 1), 1024 * js[0] : 1024 * (js[-1] + 1)])

        def load_x_pair(m, i, queue):
            js = pieces[m][i]
            width = 1024 * len(js)
            pair = keep.tile([P, 2, width], BF16, name="xpair_%d_%d" % (m, i))
            queue.dma_start(
                out=pair[:],
                in_=x[P * m : P * (m + 2), 1024 * js[0] : 1024 * (js[-1] + 1)].rearrange("(m p) k -> p m k", p=P),
            )
            x_sb[(m, i)] = pair[:, 0, :]
            x_sb[(m + 1, i)] = pair[:, 1, :]

        def load_w(t):
            gs = w_groups[t]
            nc.sync.dma_start(
                out=w_tiles[t][:].bitcast(I32),
                in_=weight_words[gs[0] : gs[-1] + 1].rearrange("g p n -> p g n").bitcast(I32),
            )

        def load_scales(s, queue, view):
            g0, g1 = plane_groups[s]
            for r in range(4):
                queue.dma_start(out=planes[s][r:P:32, :, :].bitcast(view), in_=scale_rows[r:16:4, g0:g1, :].bitcast(view))

        def sort_piece(m, i):
            n = len(pieces[m][i])
            ordered[(m, i)] = keep.tile([P, 2 * n, 2, P], F32, name="ordered_%d_%d" % (m, i))
            nc.vector.tensor_copy(
                out=ordered[(m, i)][:],
                in_=x_sb[(m, i)][:].bitcast(F32).rearrange("p (g j u) -> p g u j", j=P, u=2),
            )

        def transposes(m, j, bank):
            i, jj = where[(m, j)]
            banks[(m, j)] = psum.tile([P, 2, 2, P], F32, tag=bank, name="xt_%d_%d" % (m, j))
            words = x_sb[(m, i)][:].bitcast(F32)
            for gg in range(2):
                for u in range(2):
                    c0 = 256 * (2 * jj + gg)
                    if (m, i) in ordered:
                        nc.tensor.transpose(banks[(m, j)][:, gg, u, :], ordered[(m, i)][:, 2 * jj + gg, u, :], ident[:])
                    else:
                        nc.tensor.transpose(banks[(m, j)][:, gg, u, :], words[:, c0 + u : c0 + 256 : 2], ident[:])

        def copy_out(m, j, engine):
            grouped[(m, j)] = keep.tile([P, 2, P, 4], BF16, name="grouped_%d_%d" % (m, j), align_bytes=64)
            source = banks[(m, j)][:].rearrange("p g u r -> p g r u")
            if engine == 0:
                nc.scalar.copy(out=grouped[(m, j)][:].bitcast(F32), in_=source)
            else:
                nc.vector.tensor_copy(out=grouped[(m, j)][:].bitcast(F32), in_=source)

        def quantise(m, j):
            codes[(m, j)] = keep.tile([P, 2, P], U32, name="codes_%d_%d" % (m, j), align_bytes=64)
            x_planes[(m, j)] = keep.tile([P, 2, P], U8, name="x_planes_%d_%d" % (m, j), align_bytes=64)
            nc.vector.quantize_mx(
                out=codes[(m, j)][:].rearrange("p g r -> p (g r)").bitcast(FP8X4),
                scales=x_planes[(m, j)][:].rearrange("p g r -> p (g r)"),
                in_=grouped[(m, j)][:].rearrange("p g r t -> p (g r t)"),
            )

        def mx_pass(m, h, g, c0, c1):
            if g == 0 and c0 == 0:
                acc[(m, h)] = psum.tile([P, NH], F32, tag="a%d" % (2 * (m % 2) + h), name="acc_%d_%d" % (m, h))
            s, gl = plane_of[g]
            nc.tensor.matmul_mx(
                out=acc[(m, h)][:, c0:c1],
                lhsT=codes[(m, g // 2)][:, g % 2, :].bitcast(FP8X4),
                lhsT_scale=x_planes[(m, g // 2)][:, g % 2, :],
                rhs=w_words[g][:, 2 * (NH * h + c0) : 2 * (NH * h + c1)].bitcast(FP4X4),
                rhs_scale=planes[s][:, gl, NH * h + c0 : NH * h + c1],
                start=(g == 0),
                stop=(g == 7),
            )

        def mx_pass_narrow(m, h, g, c, bank):
            if g == 0:
                acc[(m, h, c)] = psum.tile([P, P], F32, tag=bank, name="acc_%d_%d_%d" % (m, h, c))
            s, gl = plane_of[g]
            c0 = NH * h + P * c
            nc.tensor.matmul_mx(
                out=acc[(m, h, c)][:],
                lhsT=codes[(m, g // 2)][:, g % 2, :].bitcast(FP8X4),
                lhsT_scale=x_planes[(m, g // 2)][:, g % 2, :],
                rhs=w_words[g][:, 2 * c0 : 2 * (c0 + P)].bitcast(FP4X4),
                rhs_scale=planes[s][:, gl, c0 : c0 + P],
                start=(g == 0),
                stop=(g == 7),
            )

        def finish_narrow(m, h, c, queue):
            c0 = NH * h + P * c
            narrow = keep.tile([P, P], F32, name="narrow_%d_%d_%d" % (m, h, c))
            nc.vector.tensor_tensor(out=narrow[:], in0=acc[(m, h, c)][:], in1=bias_all[:, c0 : c0 + P], op=ADD)
            queue.dma_start(out=y[P * m : P * (m + 1), c0 : c0 + P], in_=narrow[:])

        def add_bias(m, h, c0, c1):
            result[(m, h, c0)] = keep.tile([P, c1 - c0], F32, name="result_%d_%d_%d" % (m, h, c0))
            nc.vector.tensor_tensor(
                out=result[(m, h, c0)][:], in0=acc[(m, h)][:, c0:c1], in1=bias_all[:, NH * h + c0 : NH * h + c1], op=ADD
            )

        def store(m, h, c0, c1, queue):
            queue.dma_start(out=y[P * m : P * (m + 1), NH * h + c0 : NH * h + c1], in_=result[(m, h, c0)][:])

        def spread_bias(h, bank, engine):
            spread = psum.tile([P, NH], F32, tag=bank, name="spread_%d" % h)
            nc.tensor.matmul(out=spread[:], lhsT=ones[:], rhs=bias_row[:, NH * h : NH * (h + 1)], start=True, stop=True)
            if engine == 0:
                nc.scalar.copy(out=bias_all[:, NH * h : NH * (h + 1)], in_=spread[:])
            else:
                nc.vector.tensor_copy(out=bias_all[:, NH * h : NH * (h + 1)], in_=spread[:])

        nc.vector.memset(bias_row[:], 0.0)
        zero_planes(0)
        zero_planes(1)
        zero_planes(2)
        nc.vector.memset(ones[:], 1.0)
        make_identity(nc, ident[:])
        nc.scalar.dma_start(out=bias_row[0:1, :], in_=bias.rearrange("(o n) -> o n", o=1))
        load_x(0, 0, nc.sync)
        load_x(1, 0, nc.sync)
        load_scales(0, nc.sync, I32)
        load_w(0)
        load_x(0, 1, nc.sync)
        load_x(1, 1, nc.sync)
        load_w(1)
        load_scales(1, nc.sync, I32)
        load_w(2)
        load_w(3)
        load_x(0, 2, nc.sync)
        load_x(1, 2, nc.sync)
        load_scales(2, nc.sync, I32)
        load_w(4)
        load_w(5)
        load_w(6)
        load_x(2, 0, nc.sync)
        load_x(2, 1, nc.sync)
        load_w(7)
        load_x(3, 0, nc.sync)
        load_x(3, 1, nc.sync)
        transposes(0, 0, "t0")
        copy_out(0, 0, 0)
        quantise(0, 0)
        transposes(1, 0, "t1")
        copy_out(1, 0, 0)
        quantise(1, 0)
        mx_pass(0, 0, 0, 0, 512)
        mx_pass(0, 1, 0, 0, 512)
        mx_pass(1, 0, 0, 0, 512)
        mx_pass(1, 1, 0, 0, 512)
        transposes(0, 1, "t2")
        copy_out(0, 1, 0)
        quantise(0, 1)
        transposes(1, 1, "t3")
        copy_out(1, 1, 0)
        quantise(1, 1)
        mx_pass(0, 0, 1, 0, 512)
        mx_pass(0, 1, 1, 0, 512)
        mx_pass(1, 0, 1, 0, 512)
        mx_pass(1, 1, 1, 0, 512)
        mx_pass(0, 0, 2, 0, 512)
        mx_pass(0, 1, 2, 0, 512)
        mx_pass(1, 0, 2, 0, 512)
        mx_pass(1, 1, 2, 0, 512)
        mx_pass(0, 0, 3, 0, 512)
        mx_pass(0, 1, 3, 0, 512)
        mx_pass(1, 0, 3, 0, 512)
        mx_pass(1, 1, 3, 0, 512)
        sort_piece(0, 2)
        sort_piece(1, 2)
        transposes(0, 2, "t0")
        copy_out(0, 2, 0)
        transposes(0, 3, "t1")
        copy_out(0, 3, 1)
        quantise(0, 2)
        quantise(0, 3)
        transposes(1, 2, "t2")
        copy_out(1, 2, 0)
        transposes(1, 3, "t3")
        copy_out(1, 3, 0)
        quantise(1, 2)
        quantise(1, 3)
        spread_bias(0, "t0", 0)
        spread_bias(1, "t1", 1)
        mx_pass(0, 0, 4, 0, 512)
        mx_pass(0, 1, 4, 0, 512)
        mx_pass(1, 0, 4, 0, 512)
        mx_pass(1, 1, 4, 0, 512)
        mx_pass(0, 0, 5, 0, 512)
        mx_pass(0, 1, 5, 0, 512)
        mx_pass(1, 0, 5, 0, 512)
        mx_pass(1, 1, 5, 0, 512)
        mx_pass(0, 0, 6, 0, 512)
        mx_pass(0, 1, 6, 0, 512)
        mx_pass(1, 0, 6, 0, 512)
        mx_pass(1, 1, 6, 0, 512)
        sort_piece(2, 0)
        sort_piece(2, 1)
        transposes(2, 0, "t2")
        copy_out(2, 0, 0)
        transposes(2, 1, "t3")
        copy_out(2, 1, 0)
        transposes(2, 2, "t0")
        copy_out(2, 2, 0)
        transposes(2, 3, "t1")
        copy_out(2, 3, 0)
        quantise(2, 0)
        quantise(2, 1)
        mx_pass(0, 0, 7, 0, 512)
        mx_pass(0, 1, 7, 0, 512)
        mx_pass(1, 0, 7, 0, 512)
        mx_pass(1, 1, 7, 0, 512)
        add_bias(0, 0, 0, 512)
        store(0, 0, 0, 512, nc.sync)
        add_bias(0, 1, 0, 512)
        store(0, 1, 0, 512, nc.sync)
        quantise(2, 2)
        quantise(2, 3)
        sort_piece(3, 0)
        sort_piece(3, 1)
        add_bias(1, 0, 0, 512)
        store(1, 0, 0, 512, nc.sync)
        add_bias(1, 1, 0, 512)
        store(1, 1, 0, 512, nc.sync)
        mx_pass(2, 0, 0, 0, 512)
        mx_pass(2, 0, 1, 0, 512)
        mx_pass(2, 0, 2, 0, 512)
        mx_pass(2, 0, 3, 0, 512)
        mx_pass(2, 0, 4, 0, 512)
        mx_pass(2, 0, 5, 0, 512)
        mx_pass(2, 0, 6, 0, 512)
        mx_pass(2, 0, 7, 0, 512)
        add_bias(2, 0, 0, 512)
        store(2, 0, 0, 512, nc.sync)
        transposes(3, 0, "t2")
        copy_out(3, 0, 0)
        transposes(3, 1, "t3")
        copy_out(3, 1, 0)
        transposes(3, 2, "t0")
        copy_out(3, 2, 0)
        transposes(3, 3, "t1")
        copy_out(3, 3, 0)
        quantise(3, 0)
        quantise(3, 1)
        quantise(3, 2)
        quantise(3, 3)
        mx_pass(2, 1, 0, 0, 512)
        mx_pass(2, 1, 1, 0, 512)
        mx_pass(2, 1, 2, 0, 512)
        mx_pass(2, 1, 3, 0, 512)
        mx_pass(2, 1, 4, 0, 512)
        mx_pass(2, 1, 5, 0, 512)
        mx_pass(2, 1, 6, 0, 512)
        mx_pass(2, 1, 7, 0, 512)
        add_bias(2, 1, 0, 512)
        store(2, 1, 0, 512, nc.sync)
        mx_pass(3, 0, 0, 0, 512)
        mx_pass(3, 0, 1, 0, 512)
        mx_pass(3, 0, 2, 0, 512)
        mx_pass(3, 0, 3, 0, 512)
        mx_pass(3, 0, 4, 0, 512)
        mx_pass(3, 0, 5, 0, 512)
        mx_pass(3, 0, 6, 0, 512)
        mx_pass(3, 0, 7, 0, 512)
        add_bias(3, 0, 0, 512)
        store(3, 0, 0, 512, nc.sync)
        mx_pass_narrow(3, 1, 0, 0, "t0")
        mx_pass_narrow(3, 1, 1, 0, "t0")
        mx_pass_narrow(3, 1, 2, 0, "t0")
        mx_pass_narrow(3, 1, 3, 0, "t0")
        mx_pass_narrow(3, 1, 4, 0, "t0")
        mx_pass_narrow(3, 1, 5, 0, "t0")
        mx_pass_narrow(3, 1, 6, 0, "t0")
        mx_pass_narrow(3, 1, 7, 0, "t0")
        finish_narrow(3, 1, 0, nc.sync)
        mx_pass_narrow(3, 1, 0, 1, "t1")
        mx_pass_narrow(3, 1, 1, 1, "t1")
        mx_pass_narrow(3, 1, 2, 1, "t1")
        mx_pass_narrow(3, 1, 3, 1, "t1")
        mx_pass_narrow(3, 1, 4, 1, "t1")
        mx_pass_narrow(3, 1, 5, 1, "t1")
        mx_pass_narrow(3, 1, 6, 1, "t1")
        mx_pass_narrow(3, 1, 7, 1, "t1")
        finish_narrow(3, 1, 1, nc.sync)
        mx_pass_narrow(3, 1, 0, 2, "t2")
        mx_pass_narrow(3, 1, 1, 2, "t2")
        mx_pass_narrow(3, 1, 2, 2, "t2")
        mx_pass_narrow(3, 1, 3, 2, "t2")
        mx_pass_narrow(3, 1, 4, 2, "t2")
        mx_pass_narrow(3, 1, 5, 2, "t2")
        mx_pass_narrow(3, 1, 6, 2, "t2")
        mx_pass_narrow(3, 1, 7, 2, "t2")
        finish_narrow(3, 1, 2, nc.sync)
        mx_pass_narrow(3, 1, 0, 3, "t3")
        mx_pass_narrow(3, 1, 1, 3, "t3")
        mx_pass_narrow(3, 1, 2, 3, "t3")
        mx_pass_narrow(3, 1, 3, 3, "t3")
        mx_pass_narrow(3, 1, 4, 3, "t3")
        mx_pass_narrow(3, 1, 5, 3, "t3")
        mx_pass_narrow(3, 1, 6, 3, "t3")
        mx_pass_narrow(3, 1, 7, 3, "t3")
        finish_narrow(3, 1, 3, nc.sync)
